import numpy as np
import ml_dtypes


def mxq(x, axis, fmt="e4m3"):
    dtype, down = {"e4m3": (ml_dtypes.float8_e4m3fn, 7), "e5m2": (ml_dtypes.float8_e5m2, 14)}[fmt]
    v = np.moveaxis(np.asarray(x, np.float32).astype(ml_dtypes.bfloat16).astype(np.float64), axis, -1)
    blocks = v.reshape(v.shape[:-1] + (-1, 32))
    amax = np.abs(blocks).max(-1, keepdims=True)
    byte = np.maximum(np.where(amax > 0, np.frexp(amax)[1] - 1 + 127, 0) - down, 1)
    scale = np.exp2(byte - 127.0)
    codes = (blocks / scale).astype(np.float32).astype(dtype).astype(np.float64)
    return np.moveaxis((codes * scale).reshape(v.shape), -1, axis)


WIDE = False


def mx_kscale(k):
    if not WIDE:
        return np.ones(k)
    levels = np.array([10, -10, 5, -5, 0])
    a = np.random.permutation(np.resize(levels, k // 512 * 4)).reshape(k // 512, 4)
    idx = np.arange(k)
    return np.exp2(a[idx // 512, idx % 128 // 32])


BF16 = ml_dtypes.bfloat16


def bf(x):
    return np.asarray(x, np.float32).astype(BF16)


def f64(x):
    return np.asarray(x).astype(np.float64)


B, T, HIDDEN, NUM_HEADS, HEAD_DIM, ROT_DIM, LATENT = 2, 64, 1024, 16, 128, 64, 512
NOPE_DIM = HEAD_DIM - ROT_DIM
BASE = 10000.0


def rope_tables():
    inv_freq = 1.0 / (BASE ** (np.arange(0, ROT_DIM, 2) / ROT_DIM))
    freqs = np.arange(T)[:, None] * inv_freq[None, :]
    emb = np.concatenate((freqs, freqs), axis=-1)
    return np.cos(emb), np.sin(emb)


def rotate_half(v):
    v1, v2 = v[..., : v.shape[-1] // 2], v[..., v.shape[-1] // 2 :]
    return np.concatenate((-v2, v1), axis=-1)


def heads(y, d):
    return y.reshape(B, T, NUM_HEADS, d).transpose(0, 2, 1, 3)


def setup_inputs():
    s, t = mx_kscale(HIDDEN), mx_kscale(LATENT)
    cos, sin = rope_tables()
    return {"x": bf(np.random.standard_normal((B, T, HIDDEN)) * s),
            "Wq_d": bf(np.random.standard_normal((HIDDEN, LATENT)) / np.sqrt(HIDDEN) / s[:, None] * t),
            "Wq_nope": bf(np.random.standard_normal((LATENT, NUM_HEADS * NOPE_DIM)) / np.sqrt(LATENT) / t[:, None]),
            "Wrq": bf(np.random.standard_normal((LATENT, NUM_HEADS * ROT_DIM)) / np.sqrt(LATENT) / t[:, None]),
            "cos": bf(cos), "sin": bf(sin)}


def reference(x, Wq_d, Wq_nope, Wrq, cos, sin):
    q_latent = mxq(f64(x), 2, "e4m3") @ mxq(f64(Wq_d), 0, "e4m3")
    lq = mxq(q_latent, 2, "e4m3")
    q_nope = heads(lq @ mxq(f64(Wq_nope), 0, "e4m3"), NOPE_DIM)
    q_rot = heads(lq @ mxq(f64(Wrq), 0, "e4m3"), ROT_DIM)
    c, sn = f64(cos)[None, None, :, :], f64(sin)[None, None, :, :]
    q_rot = q_rot * c + rotate_half(q_rot) * sn
    return np.concatenate([q_rot, q_nope], axis=-1)

@@ -1,0 +1,199 @@
+from contextlib import ExitStack
+
+import concourse.mybir as mybir
+from concourse.masks import make_identity
+
+BF16 = mybir.dt.bfloat16
+F32 = mybir.dt.float32
+U32 = mybir.dt.uint32
+U8 = mybir.dt.uint8
+FP8X4 = mybir.dt.float8_e4m3fn_x4
+MULT = mybir.AluOpType.mult
+ADD = mybir.AluOpType.add
+SUBTRACT = mybir.AluOpType.subtract
+
+P = 128
+PACK = 4
+K_PASS = P * PACK
+
+BATCH, SEQ, HIDDEN, LATENT = 2, 64, 1024, 512
+HEADS, ROT, NOPE = 16, 64, 64
+HALF = ROT // 2
+HEAD = ROT + NOPE
+UP = HEADS * ROT
+DOWN_PASSES = HIDDEN // K_PASS
+
+LOAD_COLS = 512
+PIECE = 256
+PIECE_HEADS = PIECE // ROT
+BANK_HEADS = 512 // ROT
+RUN = 4
+
+VECTOR_COLS = 128
+VECTOR_COLS_NOPE = 32
+
+FLOPS = 2 * BATCH * SEQ * (HIDDEN * LATENT + LATENT * 2 * UP)
+
+
+def regroup(nc, raw, grouped, vector_cols):
+    src = raw.rearrange("p j (c i) -> p c j i", i=RUN)
+    dst = grouped.rearrange("p (c i) j -> p c j i", i=RUN)
+    split = vector_cols // RUN
+    nc.vector.tensor_copy(out=dst[:, :split], in_=src[:, :split])
+    nc.scalar.copy(out=dst[:, split:], in_=src[:, split:])
+
+
+def quantise(nc, grouped, codes, scales):
+    nc.vector.quantize_mx(
+        out=codes.bitcast(FP8X4),
+        scales=scales,
+        in_=grouped.rearrange("p c j -> p (c j)"),
+    )
+
+
+def tile_multiheadlatentattention_pa_s_kernel(tc, x, Wq_d, Wq_nope, Wrq, cos, sin, out):
+    nc = tc.nc
+    with ExitStack() as ctx:
+        keep = ctx.enter_context(tc.tile_pool(name="keep", bufs=1))
+        psum = ctx.enter_context(tc.psum_pool(name="psum", bufs=1))
+
+        x_sb = keep.tile([P, HIDDEN], BF16)
+        for b in range(BATCH):
+            nc.sync.dma_start(out=x_sb[b:P:BATCH, :], in_=x[b])
+
+        down_raw = []
+        for g in range(DOWN_PASSES):
+            raw = keep.tile([P, PACK, LATENT], BF16, name="down_raw%d" % g)
+            rows = Wq_d[g * K_PASS : (g + 1) * K_PASS, :]
+            nc.sync.dma_start(out=raw[:], in_=rows.rearrange("(p j) c -> p j c", j=PACK))
+            down_raw.append(raw)
+
+        cos_sb = keep.tile([P, ROT], BF16)
+        sin_swapped = keep.tile([P, ROT], BF16)
+        for b in range(BATCH):
+            nc.scalar.dma_start(out=cos_sb[b:P:BATCH, :], in_=cos)
+            nc.scalar.dma_start(out=sin_swapped[b:P:BATCH, 0:HALF], in_=sin[:, HALF:ROT])
+            nc.scalar.dma_start(out=sin_swapped[b:P:BATCH, HALF:ROT], in_=sin[:, 0:HALF])
+
+        up_raw = []
+        for w_name, w in (("rot", Wrq), ("nope", Wq_nope)):
+            for c in range(UP // LOAD_COLS):
+                raw = keep.tile([P, PACK, LOAD_COLS], BF16, name="%s_raw%d" % (w_name, c))
+                cols = w[:, c * LOAD_COLS : (c + 1) * LOAD_COLS]
+                nc.sync.dma_start(out=raw[:], in_=cols.rearrange("(j p) n -> p j n", p=P))
+                up_raw.append(raw)
+
+        ident = keep.tile([P, P], F32)
+        make_identity(nc, ident[:])
+
+        x_words = x_sb[:].bitcast(F32)
+        xT_ps = psum.tile([P, DOWN_PASSES, 2, P], F32)
+        words_pass = K_PASS // 2
+        for g in range(DOWN_PASSES):
+            for u in range(2):
+                nc.tensor.transpose(
+                    xT_ps[:, g, u, :],
+                    x_words[:, g * words_pass + u : (g + 1) * words_pass : 2],
+                    ident[:],
+                )
+        x_grouped = keep.tile([P, DOWN_PASSES * P * PACK], BF16, align_bytes=64)
+        nc.scalar.copy(
+            out=x_grouped[:].bitcast(F32).rearrange("p (g m u) -> p g m u", g=DOWN_PASSES, u=2),
+            in_=xT_ps[:].rearrange("p g u m -> p g m u"),
+        )
+        x_codes = keep.tile([P, DOWN_PASSES, P], U32, align_bytes=64)
+        x_scales = keep.tile([P, DOWN_PASSES, P], U8, align_bytes=64)
+        nc.vector.quantize_mx(
+            out=x_codes[:].rearrange("p g m -> p (g m)").bitcast(FP8X4),
+            scales=x_scales[:].rearrange("p g m -> p (g m)"),
+            in_=x_grouped[:],
+        )
+
+        down_codes = keep.tile([P, DOWN_PASSES, LATENT], U32, align_bytes=64)
+        down_scales = keep.tile([P, DOWN_PASSES, LATENT], U8, align_bytes=64)
+        for g in range(DOWN_PASSES):
+            grouped = keep.tile([P, LATENT, PACK], BF16, name="down_grouped%d" % g, align_bytes=64)
+            for c0 in range(0, LATENT, PIECE):
+                piece = slice(c0, c0 + PIECE)
+                regroup(nc, down_raw[g][:, :, piece], grouped[:, piece, :], VECTOR_COLS)
+                quantise(nc, grouped[:, piece, :], down_codes[:, g, piece], down_scales[:, g, piece])
+
+        latT_ps = psum.tile([P, PACK, P], F32)
+        for j in range(PACK):
+            block = slice(j * P, (j + 1) * P)
+            for g in range(DOWN_PASSES):
+                nc.tensor.matmul_mx(
+                    out=latT_ps[:, j, :],
+                    lhsT=down_codes[:, g, block].bitcast(FP8X4),
+                    lhsT_scale=down_scales[:, g, block],
+                    rhs=x_codes[:, g, :].bitcast(FP8X4),
+                    rhs_scale=x_scales[:, g, :],
+                    start=(g == 0),
+                    stop=(g == DOWN_PASSES - 1),
+                )
+        lat_grouped = keep.tile([P, P, PACK], BF16, align_bytes=64)
+        nc.scalar.copy(out=lat_grouped[:], in_=latT_ps[:].rearrange("p j m -> p m j"))
+        lat_codes = keep.tile([P, P], U32, align_bytes=64)
+        lat_scales = keep.tile([P, P], U8, align_bytes=64)
+        quantise(nc, lat_grouped[:], lat_codes[:], lat_scales[:])
+
+        def up_product(raw, piece, acc, vector_cols, label):
+            grouped = keep.tile([P, PIECE, PACK], BF16, name="grouped_" + label, align_bytes=64)
+            codes = keep.tile([P, PIECE], U32, name="codes_" + label, align_bytes=64)
+            scales = keep.tile([P, PIECE], U8, name="scales_" + label, align_bytes=64)
+            regroup(nc, raw[:, :, piece], grouped[:], vector_cols)
+            quantise(nc, grouped[:], codes[:], scales[:])
+            nc.tensor.matmul_mx(
+                out=acc,
+                lhsT=lat_codes[:].bitcast(FP8X4),
+                lhsT_scale=lat_scales[:],
+                rhs=codes[:].bitcast(FP8X4),
+                rhs_scale=scales[:],
+                start=True,
+                stop=True,
+            )
+
+        out_sb = keep.tile([P, HEADS, HEAD], F32)
+        by_cos = keep.tile([P, HEADS, ROT], F32)
+        by_sin = keep.tile([P, HEADS, ROT], F32)
+        cos_heads = cos_sb[:].unsqueeze(1).to_broadcast([P, BANK_HEADS, ROT])
+        sin_heads = sin_swapped[:].unsqueeze(1).to_broadcast([P, BANK_HEADS, ROT])
+
+        for c in range(UP // LOAD_COLS):
+            rot_ps = psum.tile([P, LOAD_COLS], F32, name="rot_ps%d" % c)
+            for c0 in range(0, LOAD_COLS, PIECE):
+                piece = slice(c0, c0 + PIECE)
+                up_product(up_raw[c], piece, rot_ps[:, piece], VECTOR_COLS, "rot%d_%d" % (c, c0))
+            heads = slice(c * BANK_HEADS, (c + 1) * BANK_HEADS)
+            u = rot_ps[:].rearrange("p (h d) -> p h d", d=ROT)
+            nc.vector.tensor_tensor(out=by_cos[:, heads, :], in0=u, in1=cos_heads, op=MULT)
+            nc.vector.tensor_tensor(out=by_sin[:, heads, :], in0=u, in1=sin_heads, op=MULT)
+            nc.vector.tensor_tensor(
+                out=out_sb[:, heads, 0:HALF],
+                in0=by_cos[:, heads, 0:HALF],
+                in1=by_sin[:, heads, HALF:ROT],
+                op=SUBTRACT,
+            )
+            nc.vector.tensor_tensor(
+                out=out_sb[:, heads, HALF:ROT],
+                in0=by_cos[:, heads, HALF:ROT],
+                in1=by_sin[:, heads, 0:HALF],
+                op=ADD,
+            )
+
+        for c in range(UP // LOAD_COLS):
+            for c0 in range(0, LOAD_COLS, PIECE):
+                piece = slice(c0, c0 + PIECE)
+                nope_ps = psum.tile([P, PIECE], F32, name="nope_ps%d_%d" % (c, c0))
+                up_product(up_raw[2 + c], piece, nope_ps[:], VECTOR_COLS_NOPE, "nope%d_%d" % (c, c0))
+                h0 = (c * LOAD_COLS + c0) // NOPE
+                heads = slice(h0, h0 + PIECE_HEADS)
+                nc.scalar.copy(
+                    out=out_sb[:, heads, ROT:HEAD],
+                    in_=nope_ps[:].rearrange("p (h d) -> p h d", d=NOPE),
+                )
+                for b in range(BATCH):
+                    nc.sync.dma_start(
+                        out=out[b, heads].rearrange("h t d -> t h d"),
+                        in_=out_sb[b:P:BATCH, heads, :],
+                    )

@@ -18,36 +18,35 @@ K_PASS = P * PACK
 
 BATCH, SEQ, HIDDEN, LATENT = 2, 64, 1024, 512
 HEADS, ROT, NOPE = 16, 64, 64
-HALF = ROT // 2
+HALF_ROT = ROT // 2
 HEAD = ROT + NOPE
 UP = HEADS * ROT
 DOWN_PASSES = HIDDEN // K_PASS
 
-LOAD_COLS = 512
-PIECE = 256
+UNIT = 512
+PIECE = UNIT // 2
+FIRST, SECOND = slice(0, PIECE), slice(PIECE, UNIT)
+UNIT_HEADS = UNIT // ROT
 PIECE_HEADS = PIECE // ROT
-BANK_HEADS = 512 // ROT
+NOPE_PIECES = UP // PIECE
 RUN = 4
-
-VECTOR_COLS = 128
-VECTOR_COLS_NOPE = 32
+EVACUATE_BEHIND = 2
 
 FLOPS = 2 * BATCH * SEQ * (HIDDEN * LATENT + LATENT * 2 * UP)
 
 
-def regroup(nc, raw, grouped, vector_cols):
-    src = raw.rearrange("p j (c i) -> p c j i", i=RUN)
-    dst = grouped.rearrange("p (c i) j -> p c j i", i=RUN)
-    split = vector_cols // RUN
-    nc.vector.tensor_copy(out=dst[:, :split], in_=src[:, :split])
-    nc.scalar.copy(out=dst[:, split:], in_=src[:, split:])
+def regroup(copy, weight, cols):
+    copy(
+        out=weight["grouped"][:, cols, :].rearrange("p (c i) j -> p c j i", i=RUN),
+        in_=weight["raw"][:, :, cols].rearrange("p j (c i) -> p c j i", i=RUN),
+    )
 
 
-def quantise(nc, grouped, codes, scales):
+def quantise(nc, weight, cols):
     nc.vector.quantize_mx(
-        out=codes.bitcast(FP8X4),
-        scales=scales,
-        in_=grouped.rearrange("p c j -> p (c j)"),
+        out=weight["codes"][:, cols].bitcast(FP8X4),
+        scales=weight["scales"][:, cols],
+        in_=weight["grouped"][:, cols, :].rearrange("p c j -> p (c j)"),
     )
 
 
@@ -56,32 +55,37 @@ def tile_multiheadlatentattention_pa_s_kernel(tc, x, Wq_d, Wq_nope, Wrq, cos, si
     with ExitStack() as ctx:
         keep = ctx.enter_context(tc.tile_pool(name="keep", bufs=1))
         psum = ctx.enter_context(tc.psum_pool(name="psum", bufs=1))
+        ctx.enter_context(tc.manual_schedule())
+
+        def load_weight(name, rows_by_partition):
+            raw = keep.tile([P, PACK, UNIT], BF16, name=name + "_raw")
+            nc.sync.dma_start(out=raw[:], in_=rows_by_partition)
+            return {
+                "raw": raw,
+                "grouped": keep.tile([P, UNIT, PACK], BF16, name=name + "_grouped", align_bytes=64),
+                "codes": keep.tile([P, UNIT], U32, name=name + "_codes", align_bytes=64),
+                "scales": keep.tile([P, UNIT], U8, name=name + "_scales", align_bytes=64),
+            }
 
         x_sb = keep.tile([P, HIDDEN], BF16)
         for b in range(BATCH):
             nc.sync.dma_start(out=x_sb[b:P:BATCH, :], in_=x[b])
-
-        down_raw = []
+        down = []
         for g in range(DOWN_PASSES):
-            raw = keep.tile([P, PACK, LATENT], BF16, name="down_raw%d" % g)
             rows = Wq_d[g * K_PASS : (g + 1) * K_PASS, :]
-            nc.sync.dma_start(out=raw[:], in_=rows.rearrange("(p j) c -> p j c", j=PACK))
-            down_raw.append(raw)
-
+            down.append(load_weight("down%d" % g, rows.rearrange("(p j) c -> p j c", j=PACK)))
         cos_sb = keep.tile([P, ROT], BF16)
         sin_swapped = keep.tile([P, ROT], BF16)
         for b in range(BATCH):
             nc.scalar.dma_start(out=cos_sb[b:P:BATCH, :], in_=cos)
-            nc.scalar.dma_start(out=sin_swapped[b:P:BATCH, 0:HALF], in_=sin[:, HALF:ROT])
-            nc.scalar.dma_start(out=sin_swapped[b:P:BATCH, HALF:ROT], in_=sin[:, 0:HALF])
-
-        up_raw = []
-        for w_name, w in (("rot", Wrq), ("nope", Wq_nope)):
-            for c in range(UP // LOAD_COLS):
-                raw = keep.tile([P, PACK, LOAD_COLS], BF16, name="%s_raw%d" % (w_name, c))
-                cols = w[:, c * LOAD_COLS : (c + 1) * LOAD_COLS]
-                nc.sync.dma_start(out=raw[:], in_=cols.rearrange("(j p) n -> p j n", p=P))
-                up_raw.append(raw)
+            nc.scalar.dma_start(out=sin_swapped[b:P:BATCH, 0:HALF_ROT], in_=sin[:, HALF_ROT:ROT])
+            nc.scalar.dma_start(out=sin_swapped[b:P:BATCH, HALF_ROT:ROT], in_=sin[:, 0:HALF_ROT])
+        rot = []
+        nope = []
+        for name, w, units in (("rot", Wrq, rot), ("nope", Wq_nope, nope)):
+            for c in range(UP // UNIT):
+                cols = w[:, c * UNIT : (c + 1) * UNIT]
+                units.append(load_weight("%s%d" % (name, c), cols.rearrange("(j p) n -> p j n", p=P)))
 
         ident = keep.tile([P, P], F32)
         make_identity(nc, ident[:])
@@ -103,20 +107,20 @@ def tile_multiheadlatentattention_pa_s_kernel(tc, x, Wq_d, Wq_nope, Wrq, cos, si
         )
         x_codes = keep.tile([P, DOWN_PASSES, P], U32, align_bytes=64)
         x_scales = keep.tile([P, DOWN_PASSES, P], U8, align_bytes=64)
+
+        regroup(nc.vector.tensor_copy, down[0], FIRST)
+        regroup(nc.scalar.copy, down[0], SECOND)
         nc.vector.quantize_mx(
             out=x_codes[:].rearrange("p g m -> p (g m)").bitcast(FP8X4),
             scales=x_scales[:].rearrange("p g m -> p (g m)"),
             in_=x_grouped[:],
         )
-
-        down_codes = keep.tile([P, DOWN_PASSES, LATENT], U32, align_bytes=64)
-        down_scales = keep.tile([P, DOWN_PASSES, LATENT], U8, align_bytes=64)
-        for g in range(DOWN_PASSES):
-            grouped = keep.tile([P, LATENT, PACK], BF16, name="down_grouped%d" % g, align_bytes=64)
-            for c0 in range(0, LATENT, PIECE):
-                piece = slice(c0, c0 + PIECE)
-                regroup(nc, down_raw[g][:, :, piece], grouped[:, piece, :], VECTOR_COLS)
-                quantise(nc, grouped[:, piece, :], down_codes[:, g, piece], down_scales[:, g, piece])
+        quantise(nc, down[0], FIRST)
+        regroup(nc.vector.tensor_copy, down[1], FIRST)
+        regroup(nc.scalar.copy, down[1], SECOND)
+        quantise(nc, down[0], SECOND)
+        quantise(nc, down[1], FIRST)
+        quantise(nc, down[1], SECOND)
 
         latT_ps = psum.tile([P, PACK, P], F32)
         for j in range(PACK):
@@ -124,73 +128,96 @@ def tile_multiheadlatentattention_pa_s_kernel(tc, x, Wq_d, Wq_nope, Wrq, cos, si
             for g in range(DOWN_PASSES):
                 nc.tensor.matmul_mx(
                     out=latT_ps[:, j, :],
-                    lhsT=down_codes[:, g, block].bitcast(FP8X4),
-                    lhsT_scale=down_scales[:, g, block],
+                    lhsT=down[g]["codes"][:, block].bitcast(FP8X4),
+                    lhsT_scale=down[g]["scales"][:, block],
                     rhs=x_codes[:, g, :].bitcast(FP8X4),
                     rhs_scale=x_scales[:, g, :],
                     start=(g == 0),
                     stop=(g == DOWN_PASSES - 1),
                 )
         lat_grouped = keep.tile([P, P, PACK], BF16, align_bytes=64)
-        nc.scalar.copy(out=lat_grouped[:], in_=latT_ps[:].rearrange("p j m -> p m j"))
         lat_codes = keep.tile([P, P], U32, align_bytes=64)
         lat_scales = keep.tile([P, P], U8, align_bytes=64)
-        quantise(nc, lat_grouped[:], lat_codes[:], lat_scales[:])
 
-        def up_product(raw, piece, acc, vector_cols, label):
-            grouped = keep.tile([P, PIECE, PACK], BF16, name="grouped_" + label, align_bytes=64)
-            codes = keep.tile([P, PIECE], U32, name="codes_" + label, align_bytes=64)
-            scales = keep.tile([P, PIECE], U8, name="scales_" + label, align_bytes=64)
-            regroup(nc, raw[:, :, piece], grouped[:], vector_cols)
-            quantise(nc, grouped[:], codes[:], scales[:])
+        def up_product(acc, weight, cols):
             nc.tensor.matmul_mx(
                 out=acc,
                 lhsT=lat_codes[:].bitcast(FP8X4),
                 lhsT_scale=lat_scales[:],
-                rhs=codes[:].bitcast(FP8X4),
-                rhs_scale=scales[:],
+                rhs=weight["codes"][:, cols].bitcast(FP8X4),
+                rhs_scale=weight["scales"][:, cols],
                 start=True,
                 stop=True,
             )
 
+        regroup(nc.vector.tensor_copy, rot[0], FIRST)
+        regroup(nc.scalar.copy, rot[0], SECOND)
+        nc.scalar.copy(out=lat_grouped[:], in_=latT_ps[:].rearrange("p j m -> p m j"))
+        quantise(nc, rot[0], FIRST)
+        regroup(nc.vector.tensor_copy, rot[1], FIRST)
+        regroup(nc.scalar.copy, rot[1], SECOND)
+        quantise(nc, rot[0], SECOND)
+        nc.vector.quantize_mx(
+            out=lat_codes[:].bitcast(FP8X4),
+            scales=lat_scales[:],
+            in_=lat_grouped[:].rearrange("p m j -> p (m j)"),
+        )
+        quantise(nc, rot[1], FIRST)
+        quantise(nc, rot[1], SECOND)
+        rot_ps = []
+        for c in range(UP // UNIT):
+            acc = psum.tile([P, UNIT], F32, name="rot_ps%d" % c)
+            for cols in (FIRST, SECOND):
+                up_product(acc[:, cols], rot[c], cols)
+            rot_ps.append(acc)
+
         out_sb = keep.tile([P, HEADS, HEAD], F32)
         by_cos = keep.tile([P, HEADS, ROT], F32)
         by_sin = keep.tile([P, HEADS, ROT], F32)
-        cos_heads = cos_sb[:].unsqueeze(1).to_broadcast([P, BANK_HEADS, ROT])
-        sin_heads = sin_swapped[:].unsqueeze(1).to_broadcast([P, BANK_HEADS, ROT])
+        cos_heads = cos_sb[:].unsqueeze(1).to_broadcast([P, UNIT_HEADS, ROT])
+        sin_heads = sin_swapped[:].unsqueeze(1).to_broadcast([P, UNIT_HEADS, ROT])
 
-        for c in range(UP // LOAD_COLS):
-            rot_ps = psum.tile([P, LOAD_COLS], F32, name="rot_ps%d" % c)
-            for c0 in range(0, LOAD_COLS, PIECE):
-                piece = slice(c0, c0 + PIECE)
-                up_product(up_raw[c], piece, rot_ps[:, piece], VECTOR_COLS, "rot%d_%d" % (c, c0))
-            heads = slice(c * BANK_HEADS, (c + 1) * BANK_HEADS)
-            u = rot_ps[:].rearrange("p (h d) -> p h d", d=ROT)
+        def rotation_products(c):
+            heads = slice(c * UNIT_HEADS, (c + 1) * UNIT_HEADS)
+            u = rot_ps[c][:].rearrange("p (h d) -> p h d", d=ROT)
             nc.vector.tensor_tensor(out=by_cos[:, heads, :], in0=u, in1=cos_heads, op=MULT)
             nc.vector.tensor_tensor(out=by_sin[:, heads, :], in0=u, in1=sin_heads, op=MULT)
+
+        def rotation_sums(c):
+            heads = slice(c * UNIT_HEADS, (c + 1) * UNIT_HEADS)
             nc.vector.tensor_tensor(
-                out=out_sb[:, heads, 0:HALF],
-                in0=by_cos[:, heads, 0:HALF],
-                in1=by_sin[:, heads, HALF:ROT],
+                out=out_sb[:, heads, 0:HALF_ROT],
+                in0=by_cos[:, heads, 0:HALF_ROT],
+                in1=by_sin[:, heads, HALF_ROT:ROT],
                 op=SUBTRACT,
             )
             nc.vector.tensor_tensor(
-                out=out_sb[:, heads, HALF:ROT],
-                in0=by_cos[:, heads, HALF:ROT],
-                in1=by_sin[:, heads, 0:HALF],
+                out=out_sb[:, heads, HALF_ROT:ROT],
+                in0=by_cos[:, heads, HALF_ROT:ROT],
+                in1=by_sin[:, heads, 0:HALF_ROT],
                 op=ADD,
             )
 
-        for c in range(UP // LOAD_COLS):
-            for c0 in range(0, LOAD_COLS, PIECE):
-                piece = slice(c0, c0 + PIECE)
-                nope_ps = psum.tile([P, PIECE], F32, name="nope_ps%d_%d" % (c, c0))
-                up_product(up_raw[2 + c], piece, nope_ps[:], VECTOR_COLS_NOPE, "nope%d_%d" % (c, c0))
-                h0 = (c * LOAD_COLS + c0) // NOPE
-                heads = slice(h0, h0 + PIECE_HEADS)
+        nope_ps = []
+        for k in range(NOPE_PIECES + EVACUATE_BEHIND):
+            if k < NOPE_PIECES:
+                c, second = divmod(k, 2)
+                cols = SECOND if second else FIRST
+                regroup(nc.scalar.copy, nope[c], cols)
+                if second:
+                    rotation_sums(c)
+                else:
+                    rotation_products(c)
+                quantise(nc, nope[c], cols)
+                acc = psum.tile([P, PIECE], F32, name="nope_ps%d" % k)
+                up_product(acc[:], nope[c], cols)
+                nope_ps.append(acc)
+            if k >= EVACUATE_BEHIND:
+                done = k - EVACUATE_BEHIND
+                heads = slice(done * PIECE_HEADS, (done + 1) * PIECE_HEADS)
                 nc.scalar.copy(
                     out=out_sb[:, heads, ROT:HEAD],
-                    in_=nope_ps[:].rearrange("p (h d) -> p h d", d=NOPE),
+                    in_=nope_ps[done][:].rearrange("p (h d) -> p h d", d=NOPE),
                 )
                 for b in range(BATCH):
                     nc.sync.dma_start(

@@ -74,12 +74,6 @@ def tile_multiheadlatentattention_pa_s_kernel(tc, x, Wq_d, Wq_nope, Wrq, cos, si
         for g in range(DOWN_PASSES):
             rows = Wq_d[g * K_PASS : (g + 1) * K_PASS, :]
             down.append(load_weight("down%d" % g, rows.rearrange("(p j) c -> p j c", j=PACK)))
-        cos_sb = keep.tile([P, ROT], BF16)
-        sin_swapped = keep.tile([P, ROT], BF16)
-        for b in range(BATCH):
-            nc.scalar.dma_start(out=cos_sb[b:P:BATCH, :], in_=cos)
-            nc.scalar.dma_start(out=sin_swapped[b:P:BATCH, 0:HALF_ROT], in_=sin[:, HALF_ROT:ROT])
-            nc.scalar.dma_start(out=sin_swapped[b:P:BATCH, HALF_ROT:ROT], in_=sin[:, 0:HALF_ROT])
         rot = []
         nope = []
         for name, w, units in (("rot", Wrq, rot), ("nope", Wq_nope, nope)):
@@ -89,6 +83,14 @@ def tile_multiheadlatentattention_pa_s_kernel(tc, x, Wq_d, Wq_nope, Wrq, cos, si
 
         ident = keep.tile([P, P], F32)
         make_identity(nc, ident[:])
+
+        cos_sb = keep.tile([P, ROT], BF16)
+        sin_swapped = keep.tile([P, ROT], BF16)
+        for b in range(BATCH):
+            nc.gpsimd.dma_start(out=cos_sb[b:P:BATCH, :], in_=cos)
+        for b in range(BATCH):
+            nc.gpsimd.dma_start(out=sin_swapped[b:P:BATCH, 0:HALF_ROT], in_=sin[:, HALF_ROT:ROT])
+            nc.gpsimd.dma_start(out=sin_swapped[b:P:BATCH, HALF_ROT:ROT], in_=sin[:, 0:HALF_ROT])
 
         x_words = x_sb[:].bitcast(F32)
         xT_ps = psum.tile([P, DOWN_PASSES, 2, P], F32)

from contextlib import ExitStack

import concourse.mybir as mybir
from concourse.masks import make_identity

BF16 = mybir.dt.bfloat16
F32 = mybir.dt.float32
U32 = mybir.dt.uint32
U8 = mybir.dt.uint8
FP8X4 = mybir.dt.float8_e4m3fn_x4
MULT = mybir.AluOpType.mult
ADD = mybir.AluOpType.add
SUBTRACT = mybir.AluOpType.subtract

P = 128
PACK = 4
K_PASS = P * PACK

BATCH, SEQ, HIDDEN, LATENT = 2, 64, 1024, 512
HEADS, ROT, NOPE = 16, 64, 64
HALF_ROT = ROT // 2
HEAD = ROT + NOPE
UP = HEADS * ROT
DOWN_PASSES = HIDDEN // K_PASS

UNIT = 512
PIECE = UNIT // 2
FIRST, SECOND = slice(0, PIECE), slice(PIECE, UNIT)
UNIT_HEADS = UNIT // ROT
PIECE_HEADS = PIECE // ROT
NOPE_PIECES = UP // PIECE
RUN = 4
EVACUATE_BEHIND = 2

FLOPS = 2 * BATCH * SEQ * (HIDDEN * LATENT + LATENT * 2 * UP)


def regroup(copy, weight, cols):
    copy(
        out=weight["grouped"][:, cols, :].rearrange("p (c i) j -> p c j i", i=RUN),
        in_=weight["raw"][:, :, cols].rearrange("p j (c i) -> p c j i", i=RUN),
    )


def quantise(nc, weight, cols):
    nc.vector.quantize_mx(
        out=weight["codes"][:, cols].bitcast(FP8X4),
        scales=weight["scales"][:, cols],
        in_=weight["grouped"][:, cols, :].rearrange("p c j -> p (c j)"),
    )


def tile_multiheadlatentattention_pa_s_kernel(tc, x, Wq_d, Wq_nope, Wrq, cos, sin, out):
    nc = tc.nc
    with ExitStack() as ctx:
        keep = ctx.enter_context(tc.tile_pool(name="keep", bufs=1))
        psum = ctx.enter_context(tc.psum_pool(name="psum", bufs=1))
        ctx.enter_context(tc.manual_schedule())

        def load_weight(name, rows_by_partition):
            raw = keep.tile([P, PACK, UNIT], BF16, name=name + "_raw")
            nc.sync.dma_start(out=raw[:], in_=rows_by_partition)
            return {
                "raw": raw,
                "grouped": keep.tile([P, UNIT, PACK], BF16, name=name + "_grouped", align_bytes=64),
                "codes": keep.tile([P, UNIT], U32, name=name + "_codes", align_bytes=64),
                "scales": keep.tile([P, UNIT], U8, name=name + "_scales", align_bytes=64),
            }

        x_sb = keep.tile([P, HIDDEN], BF16)
        for b in range(BATCH):
            nc.sync.dma_start(out=x_sb[b:P:BATCH, :], in_=x[b])
        down = []
        for g in range(DOWN_PASSES):
            rows = Wq_d[g * K_PASS : (g + 1) * K_PASS, :]
            down.append(load_weight("down%d" % g, rows.rearrange("(p j) c -> p j c", j=PACK)))
        rot = []
        nope = []
        for name, w, units in (("rot", Wrq, rot), ("nope", Wq_nope, nope)):
            for c in range(UP // UNIT):
                cols = w[:, c * UNIT : (c + 1) * UNIT]
                units.append(load_weight("%s%d" % (name, c), cols.rearrange("(j p) n -> p j n", p=P)))

        ident = keep.tile([P, P], F32)
        make_identity(nc, ident[:])

        cos_sb = keep.tile([P, ROT], BF16)
        sin_swapped = keep.tile([P, ROT], BF16)
        for b in range(BATCH):
            nc.gpsimd.dma_start(out=cos_sb[b:P:BATCH, :], in_=cos)
        for b in range(BATCH):
            nc.gpsimd.dma_start(out=sin_swapped[b:P:BATCH, 0:HALF_ROT], in_=sin[:, HALF_ROT:ROT])
            nc.gpsimd.dma_start(out=sin_swapped[b:P:BATCH, HALF_ROT:ROT], in_=sin[:, 0:HALF_ROT])

        x_words = x_sb[:].bitcast(F32)
        xT_ps = psum.tile([P, DOWN_PASSES, 2, P], F32)
        words_pass = K_PASS // 2
        for g in range(DOWN_PASSES):
            for u in range(2):
                nc.tensor.transpose(
                    xT_ps[:, g, u, :],
                    x_words[:, g * words_pass + u : (g + 1) * words_pass : 2],
                    ident[:],
                )
        x_grouped = keep.tile([P, DOWN_PASSES * P * PACK], BF16, align_bytes=64)
        nc.scalar.copy(
            out=x_grouped[:].bitcast(F32).rearrange("p (g m u) -> p g m u", g=DOWN_PASSES, u=2),
            in_=xT_ps[:].rearrange("p g u m -> p g m u"),
        )
        x_codes = keep.tile([P, DOWN_PASSES, P], U32, align_bytes=64)
        x_scales = keep.tile([P, DOWN_PASSES, P], U8, align_bytes=64)

        regroup(nc.vector.tensor_copy, down[0], FIRST)
        regroup(nc.scalar.copy, down[0], SECOND)
        nc.vector.quantize_mx(
            out=x_codes[:].rearrange("p g m -> p (g m)").bitcast(FP8X4),
            scales=x_scales[:].rearrange("p g m -> p (g m)"),
            in_=x_grouped[:],
        )
        quantise(nc, down[0], FIRST)
        regroup(nc.vector.tensor_copy, down[1], FIRST)
        regroup(nc.scalar.copy, down[1], SECOND)
        quantise(nc, down[0], SECOND)
        quantise(nc, down[1], FIRST)
        quantise(nc, down[1], SECOND)

        latT_ps = psum.tile([P, PACK, P], F32)
        for j in range(PACK):
            block = slice(j * P, (j + 1) * P)
            for g in range(DOWN_PASSES):
                nc.tensor.matmul_mx(
                    out=latT_ps[:, j, :],
                    lhsT=down[g]["codes"][:, block].bitcast(FP8X4),
                    lhsT_scale=down[g]["scales"][:, block],
                    rhs=x_codes[:, g, :].bitcast(FP8X4),
                    rhs_scale=x_scales[:, g, :],
                    start=(g == 0),
                    stop=(g == DOWN_PASSES - 1),
                )
        lat_grouped = keep.tile([P, P, PACK], BF16, align_bytes=64)
        lat_codes = keep.tile([P, P], U32, align_bytes=64)
        lat_scales = keep.tile([P, P], U8, align_bytes=64)

        def up_product(acc, weight, cols):
            nc.tensor.matmul_mx(
                out=acc,
                lhsT=lat_codes[:].bitcast(FP8X4),
                lhsT_scale=lat_scales[:],
                rhs=weight["codes"][:, cols].bitcast(FP8X4),
                rhs_scale=weight["scales"][:, cols],
                start=True,
                stop=True,
            )

        regroup(nc.vector.tensor_copy, rot[0], FIRST)
        regroup(nc.scalar.copy, rot[0], SECOND)
        nc.scalar.copy(out=lat_grouped[:], in_=latT_ps[:].rearrange("p j m -> p m j"))
        quantise(nc, rot[0], FIRST)
        regroup(nc.vector.tensor_copy, rot[1], FIRST)
        regroup(nc.scalar.copy, rot[1], SECOND)
        quantise(nc, rot[0], SECOND)
        nc.vector.quantize_mx(
            out=lat_codes[:].bitcast(FP8X4),
            scales=lat_scales[:],
            in_=lat_grouped[:].rearrange("p m j -> p (m j)"),
        )
        quantise(nc, rot[1], FIRST)
        quantise(nc, rot[1], SECOND)
        rot_ps = []
        for c in range(UP // UNIT):
            acc = psum.tile([P, UNIT], F32, name="rot_ps%d" % c)
            for cols in (FIRST, SECOND):
                up_product(acc[:, cols], rot[c], cols)
            rot_ps.append(acc)

        out_sb = keep.tile([P, HEADS, HEAD], F32)
        by_cos = keep.tile([P, HEADS, ROT], F32)
        by_sin = keep.tile([P, HEADS, ROT], F32)
        cos_heads = cos_sb[:].unsqueeze(1).to_broadcast([P, UNIT_HEADS, ROT])
        sin_heads = sin_swapped[:].unsqueeze(1).to_broadcast([P, UNIT_HEADS, ROT])

        def rotation_products(c):
            heads = slice(c * UNIT_HEADS, (c + 1) * UNIT_HEADS)
            u = rot_ps[c][:].rearrange("p (h d) -> p h d", d=ROT)
            nc.vector.tensor_tensor(out=by_cos[:, heads, :], in0=u, in1=cos_heads, op=MULT)
            nc.vector.tensor_tensor(out=by_sin[:, heads, :], in0=u, in1=sin_heads, op=MULT)

        def rotation_sums(c):
            heads = slice(c * UNIT_HEADS, (c + 1) * UNIT_HEADS)
            nc.vector.tensor_tensor(
                out=out_sb[:, heads, 0:HALF_ROT],
                in0=by_cos[:, heads, 0:HALF_ROT],
                in1=by_sin[:, heads, HALF_ROT:ROT],
                op=SUBTRACT,
            )
            nc.vector.tensor_tensor(
                out=out_sb[:, heads, HALF_ROT:ROT],
                in0=by_cos[:, heads, HALF_ROT:ROT],
                in1=by_sin[:, heads, 0:HALF_ROT],
                op=ADD,
            )

        nope_ps = []
        for k in range(NOPE_PIECES + EVACUATE_BEHIND):
            if k < NOPE_PIECES:
                c, second = divmod(k, 2)
                cols = SECOND if second else FIRST
                regroup(nc.scalar.copy, nope[c], cols)
                if second:
                    rotation_sums(c)
                else:
                    rotation_products(c)
                quantise(nc, nope[c], cols)
                acc = psum.tile([P, PIECE], F32, name="nope_ps%d" % k)
                up_product(acc[:], nope[c], cols)
                nope_ps.append(acc)
            if k >= EVACUATE_BEHIND:
                done = k - EVACUATE_BEHIND
                heads = slice(done * PIECE_HEADS, (done + 1) * PIECE_HEADS)
                nc.scalar.copy(
                    out=out_sb[:, heads, ROT:HEAD],
                    in_=nope_ps[done][:].rearrange("p (h d) -> p h d", d=NOPE),
                )
                for b in range(BATCH):
                    nc.sync.dma_start(
                        out=out[b, heads].rearrange("h t d -> t h d"),
                        in_=out_sb[b:P:BATCH, heads, :],
                    )
